import numpy as np
import ml_dtypes


def mxq(x, axis, fmt="e4m3"):
    dtype, down = {"e4m3": (ml_dtypes.float8_e4m3fn, 7), "e5m2": (ml_dtypes.float8_e5m2, 14)}[fmt]
    v = np.moveaxis(np.asarray(x, np.float32).astype(ml_dtypes.bfloat16).astype(np.float64), axis, -1)
    blocks = v.reshape(v.shape[:-1] + (-1, 32))
    amax = np.abs(blocks).max(-1, keepdims=True)
    byte = np.maximum(np.where(amax > 0, np.frexp(amax)[1] - 1 + 127, 0) - down, 1)
    scale = np.exp2(byte - 127.0)
    codes = (blocks / scale).astype(np.float32).astype(dtype).astype(np.float64)
    return np.moveaxis((codes * scale).reshape(v.shape), -1, axis)


WIDE = False


def mx_kscale(k):
    if not WIDE:
        return np.ones(k)
    levels = np.array([10, -10, 5, -5, 0])
    a = np.random.permutation(np.resize(levels, k // 512 * 4)).reshape(k // 512, 4)
    idx = np.arange(k)
    return np.exp2(a[idx // 512, idx % 128 // 32])


BF16 = ml_dtypes.bfloat16


def bf(x):
    return np.asarray(x, np.float32).astype(BF16)


def f64(x):
    return np.asarray(x).astype(np.float64)


B, N, G, L = 8192, 256, 64, 256
N2 = 2 * N
L2 = 2 * L
L_LIMIT = 1.0


def relu(v):
    return np.maximum(v, 0.0)


def setup_inputs():
    s, t = mx_kscale(N2), mx_kscale(L2)
    return {
        "Volt": bf(np.random.standard_normal((B, N2)) * s),
        "IM": bf(np.random.standard_normal((L2, N2)) / np.sqrt(N2) / s[None, :] * t[:, None]),
        "Ybr": bf(np.random.standard_normal((L2, L2)) / np.sqrt(L2) / t[None, :]),
        "n_o_mu_i_u": bf(np.random.standard_normal((B, L))),
    }


def reference(Volt, IM, Ybr, n_o_mu_i_u):
    mu = f64(n_o_mu_i_u)
    dv = mxq(f64(Volt), 1, "e4m3") @ mxq(f64(IM), 1, "e4m3").T
    Ibr = mxq(dv, 1, "e4m3") @ mxq(f64(Ybr), 1, "e4m3").T
    i_up = Ibr[:, :L] ** 2 + Ibr[:, L:] ** 2 - L_LIMIT ** 2
    out = np.sum(relu(i_up), axis=1)
    out = out + np.sum(np.abs(mu * i_up), axis=1)
    out = out + np.sum(relu(-mu), axis=1)
    return out

@@ -1,0 +1,330 @@
+from contextlib import ExitStack
+
+import concourse.mybir as mybir
+from concourse.masks import make_identity
+
+F32 = mybir.dt.float32
+BF16 = mybir.dt.bfloat16
+U32 = mybir.dt.uint32
+U8 = mybir.dt.uint8
+I32 = mybir.dt.int32
+FP8X4 = mybir.dt.float8_e4m3fn_x4
+ALU = mybir.AluOpType
+ACT = mybir.ActivationFunctionType
+
+B, N2, L2, L = 8192, 512, 512, 256
+P = 128
+NT = B // P
+NPAIR = NT // 2
+FLOPS = 2 * B * N2 * L2 + 2 * B * L2 * L2
+
+MANUAL = True
+D1 = 3
+D2 = 2
+E = D1 + D2 + 1
+MCH = 8
+VOLT_CUTS = [0, 2, 4] + list(range(8, NT + 1, 4))
+
+
+def tile_pinnlayer_pa_t_kernel(tc, Volt, IM, Ybr, n_o_mu_i_u, out):
+    nc = tc.nc
+    volt_v = Volt.rearrange("(p t) n -> p t n", t=NT)
+    mu_v = n_o_mu_i_u.rearrange("(p t) l -> p t l", t=NT)
+    out_v = out.rearrange("(p t) -> p t", t=NT)
+    im_v = IM.rearrange("(m t) n -> m t n", t=4)
+
+    with ExitStack() as ctx:
+        if MANUAL:
+            ctx.enter_context(tc.manual_schedule())
+        const = ctx.enter_context(tc.tile_pool(name="const", bufs=1))
+        work = ctx.enter_context(tc.tile_pool(name="work", bufs=2))
+        psum = ctx.enter_context(tc.psum_pool(name="psum", bufs=2))
+
+        im_sb = [const.tile([P, 2, N2], BF16, name="im_sb%d" % h) for h in range(2)]
+        y_sb = const.tile([P, 4, L2], BF16, name="y_sb")
+        nvc = len(VOLT_CUTS) - 1
+        volt_sb = [
+            const.tile([P, VOLT_CUTS[c + 1] - VOLT_CUTS[c], N2], BF16, name="volt%d" % c) for c in range(nvc)
+        ]
+        volt_of = {}
+        for c in range(nvc):
+            for j in range(VOLT_CUTS[c + 1] - VOLT_CUTS[c]):
+                volt_of[VOLT_CUTS[c] + j] = (c, j)
+        mu_sb = [const.tile([P, MCH, L], BF16, name="mu%d" % c) for c in range(NT // MCH)]
+
+        def load_volt(c):
+            nc.sync.dma_start(out=volt_sb[c][:], in_=volt_v[:, VOLT_CUTS[c]:VOLT_CUTS[c + 1], :])
+
+        def load_mu(c):
+            nc.sync.dma_start(out=mu_sb[c][:], in_=mu_v[:, c * MCH:(c + 1) * MCH, :])
+
+        for h in range(2):
+            nc.sync.dma_start(out=im_sb[h][:], in_=im_v[:, 2 * h:2 * h + 2, :])
+        load_volt(0)
+        load_volt(1)
+        load_volt(2)
+        nc.sync.dma_start(out=y_sb[:], in_=Ybr.rearrange("(c r) j -> r c j", r=P))
+        nmu = 0
+        for c in range(3, nvc):
+            load_volt(c)
+            if nmu < NT // MCH:
+                load_mu(nmu)
+                nmu += 1
+
+        ident = const.tile([P, P], F32, name="ident")
+        make_identity(nc, ident[:])
+
+        ssum = const.tile([P, NT], F32, name="ssum")
+        qsum = const.tile([P, NT], F32, name="qsum")
+        wneg = const.tile([P, NT], F32, name="wneg")
+        abs_sb = [const.tile([P, MCH * L // 2], I32, name="absmu%d" % c) for c in range(NT // MCH)]
+
+        im_c = const.tile([P, 512], U32, name="im_c", align_bytes=64)
+        im_s = const.tile([P, 512], U8, name="im_s", align_bytes=64)
+        y_c = const.tile([P, 512], U32, name="y_c", align_bytes=64)
+        y_s = const.tile([P, 512], U8, name="y_s", align_bytes=64)
+        im_g = const.tile([P, 2048], BF16, name="im_g", align_bytes=64)
+        y_g = const.tile([P, 2048], BF16, name="y_g", align_bytes=64)
+
+        def transpose_pair(srcs, tag, bufs):
+            tp = psum.tile([P, 2, 2, P], F32, tag=tag, name="tp_" + tag, bufs=bufs)
+            for a in range(2):
+                for u in range(2):
+                    nc.tensor.transpose(tp[:, a, u, :], srcs[a][u], ident[:])
+            return tp
+
+        def exit_pair(eng_copy, grouped, h, tp):
+            g32 = grouped[:].bitcast(F32).rearrange("p (t m u) -> p t m u", t=4, u=2)
+            eng_copy(out=g32[:, 2 * h:2 * h + 2], in_=tp[:].rearrange("p a u m -> p a m u"))
+
+        def quant_half(grouped, codes, scales, h):
+            nc.vector.quantize_mx(
+                out=codes[:, 256 * h:256 * h + 256].bitcast(FP8X4),
+                scales=scales[:, 256 * h:256 * h + 256],
+                in_=grouped[:, 1024 * h:1024 * h + 1024],
+            )
+
+        def im_src(t, u):
+            return im_sb[t // 2][:, t % 2, :].bitcast(F32)[:, u * P:(u + 1) * P]
+
+        def y_src(c, u):
+            return y_sb[:, c, :].bitcast(F32).rearrange("p (q u) -> p u q", u=2)[:, u, :]
+
+        tps, vgs, vcs, dvps, dvgs, dcs, ibps, sqs, its, qts = {}, {}, {}, {}, {}, {}, {}, {}, {}, {}
+
+        def pe_tp(m):
+            srcs = []
+            for a in range(2):
+                c, j = volt_of[2 * m + a]
+                srcs.append([volt_sb[c][:, j, :].bitcast(F32)[:, u * P:(u + 1) * P] for u in range(2)])
+            tps[m] = transpose_pair(srcs, "tp", 2)
+
+        def s_tx(m):
+            vg = work.tile([P, 1024], BF16, tag="vg", name="vg", bufs=3, align_bytes=64)
+            nc.scalar.copy(
+                out=vg[:].bitcast(F32).rearrange("p (a b u) -> p a b u", a=2, u=2),
+                in_=tps[m][:].rearrange("p a u b -> p a b u"),
+            )
+            vgs[m] = vg
+
+        def v_qv(m):
+            vc = work.tile([P, 256], U32, tag="vc", name="vc", bufs=D1 + 2, align_bytes=64)
+            vs = work.tile([P, 256], U8, tag="vs", name="vs", bufs=D1 + 2, align_bytes=64)
+            nc.vector.quantize_mx(out=vc[:].bitcast(FP8X4), scales=vs[:], in_=vgs[m][:])
+            vcs[m] = (vc, vs)
+
+        def pe_s1(m):
+            vc, vs = vcs[m]
+            dvps[m] = []
+            for a in range(2):
+                dvp = psum.tile([P, 4, P], F32, tag="dv", name="dvp", bufs=3)
+                for t in range(4):
+                    nc.tensor.matmul_mx(
+                        out=dvp[:, t, :],
+                        lhsT=im_c[:, t * P:(t + 1) * P].bitcast(FP8X4),
+                        lhsT_scale=im_s[:, t * P:(t + 1) * P],
+                        rhs=vc[:, a * P:(a + 1) * P].bitcast(FP8X4),
+                        rhs_scale=vs[:, a * P:(a + 1) * P],
+                        start=True,
+                        stop=True,
+                    )
+                dvps[m].append(dvp)
+
+        def s_dvx(m):
+            dvg = work.tile([P, 1024], BF16, tag="dvg", name="dvg", bufs=3, align_bytes=64)
+            g = dvg[:].rearrange("p (a b t) -> p a b t", a=2, t=4)
+            for a in range(2):
+                nc.scalar.copy(out=g[:, a], in_=dvps[m][a][:].rearrange("p t b -> p b t"))
+            dvgs[m] = dvg
+
+        def v_qd(m):
+            dc = work.tile([P, 256], U32, tag="dc", name="dc", bufs=D2 + 2, align_bytes=64)
+            ds = work.tile([P, 256], U8, tag="ds", name="ds", bufs=D2 + 2, align_bytes=64)
+            nc.vector.quantize_mx(out=dc[:].bitcast(FP8X4), scales=ds[:], in_=dvgs[m][:])
+            dcs[m] = (dc, ds)
+
+        def pe_s2(m):
+            dc, ds = dcs[m]
+            ibps[m] = []
+            for a in range(2):
+                ibp = psum.tile([P, 512], F32, tag="ib", name="ibp", bufs=3)
+                nc.tensor.matmul_mx(
+                    out=ibp[:],
+                    lhsT=dc[:, a * P:(a + 1) * P].bitcast(FP8X4),
+                    lhsT_scale=ds[:, a * P:(a + 1) * P],
+                    rhs=y_c[:].bitcast(FP8X4),
+                    rhs_scale=y_s[:],
+                    start=True,
+                    stop=True,
+                )
+                ibps[m].append(ibp)
+
+        def s_sq(m):
+            sq = work.tile([P, 2, 512], F32, tag="sq", name="sq", bufs=3)
+            for a in range(2):
+                nc.scalar.activation(
+                    out=sq[:, a, :],
+                    in_=ibps[m][a][:],
+                    func=ACT.Square,
+                    accum_out=ssum[:, 2 * m + a:2 * m + a + 1],
+                )
+            sqs[m] = sq
+
+        def new_epi_tiles(m):
+            its[m] = work.tile([P, 2, L], F32, tag="it", name="it", bufs=2)
+            qts[m] = work.tile([P, 2, L], F32, tag="qt", name="qt", bufs=3)
+
+        def v_i(m, lo, hi):
+            sq = sqs[m]
+            nc.vector.scalar_tensor_tensor(
+                out=its[m][:, lo:hi, :],
+                in0=sq[:, lo:hi, 0:L],
+                scalar=-1.0,
+                in1=sq[:, lo:hi, L:2 * L],
+                op0=ALU.add,
+                op1=ALU.add,
+            )
+
+        def v_q(m, lo, hi):
+            am = abs_sb[(2 * m) // MCH][:].bitcast(BF16).rearrange("p (j l) -> p j l", l=L)
+            j0 = (2 * m) % MCH
+            nc.vector.scalar_tensor_tensor(
+                out=qts[m][:, lo:hi, :],
+                in0=am[:, j0 + lo:j0 + hi, :],
+                scalar=0.5,
+                in1=its[m][:, lo:hi, :],
+                op0=ALU.add,
+                op1=ALU.mult,
+            )
+
+        def v_abs(m, a):
+            junk = work.tile([P, L], F32, tag="junkf", name="junkf", bufs=2)
+            nc.vector.scalar_tensor_tensor(
+                out=junk[:],
+                in0=qts[m][:, a, :],
+                scalar=-1.0,
+                in1=qts[m][:, a, :],
+                op0=ALU.mult,
+                op1=ALU.max,
+                accum_out=qsum[:, 2 * m + a:2 * m + a + 1],
+            )
+
+        def v_absmu(c):
+            nc.vector.tensor_scalar(
+                out=abs_sb[c][:],
+                in0=mu_sb[c][:].rearrange("p j l -> p (j l)").bitcast(I32),
+                scalar1=0x7FFF7FFF,
+                scalar2=None,
+                op0=ALU.bitwise_and,
+            )
+
+        def v_w(tau):
+            junk = work.tile([P, L], BF16, tag="junk", name="junk", bufs=2)
+            nc.vector.tensor_scalar(
+                out=junk[:],
+                in0=mu_sb[tau // MCH][:, tau % MCH, :],
+                scalar1=0.0,
+                scalar2=None,
+                op0=ALU.min,
+                op1=ALU.add,
+                accum_out=wneg[:, tau:tau + 1],
+            )
+
+        def ok(m):
+            return 0 <= m < NPAIR
+
+        for h in range(2):
+            tp = transpose_pair([[im_src(2 * h + a, u) for u in range(2)] for a in range(2)], "dv", 3)
+            exit_pair(nc.vector.tensor_copy if h == 0 else nc.scalar.copy, im_g, h, tp)
+            if h == 0:
+                quant_half(im_g, im_c, im_s, 0)
+        quant_half(im_g, im_c, im_s, 1)
+
+        w_next = [0]
+
+        def mu_work(k):
+            done = []
+            for r in range(k):
+                tau = w_next[0]
+                if tau < NT:
+                    if tau % MCH == 0:
+                        v_absmu(tau // MCH)
+                    v_w(tau)
+                    w_next[0] = tau + 1
+                    done.append(tau)
+            return done
+
+        for n in range(NPAIR + E):
+            if ok(n - D1):
+                pe_s1(n - D1)
+                s_dvx(n - D1)
+            if ok(n):
+                pe_tp(n)
+                s_tx(n)
+            if n == D1:
+                ytp = [
+                    transpose_pair([[y_src(2 * h + a, u) for u in range(2)] for a in range(2)], "ib", 3)
+                    for h in range(2)
+                ]
+            if ok(n - D1 - D2):
+                pe_s2(n - D1 - D2)
+                s_sq(n - D1 - D2)
+            m = n - E
+            last = m == NPAIR - 1
+            if ok(m) and not last:
+                new_epi_tiles(m)
+                v_i(m, 0, 2)
+            if ok(m - 1):
+                v_abs(m - 1, 0)
+            if ok(m) and not last:
+                v_q(m, 0, 2)
+            if ok(m - 1):
+                v_abs(m - 1, 1)
+            if last:
+                new_epi_tiles(m)
+                v_i(m, 0, 1)
+                v_q(m, 0, 1)
+                v_i(m, 1, 2)
+                v_abs(m, 0)
+                v_q(m, 1, 2)
+                v_abs(m, 1)
+            if ok(n - D1):
+                v_qd(n - D1)
+            if n >= 5:
+                mu_work(1)
+            if ok(n):
+                v_qv(n)
+            if n == D1:
+                for h in range(2):
+                    exit_pair(nc.vector.tensor_copy, y_g, h, ytp[h])
+                    quant_half(y_g, y_c, y_s, h)
+            if n >= 5:
+                mu_work(5 if n in (5, 6) else 1)
+
+        t1 = const.tile([P, NT], F32, name="t1")
+        res = const.tile([P, NT], F32, name="res")
+        nc.vector.scalar_tensor_tensor(out=t1[:], in0=ssum[:], scalar=0.5, in1=qsum[:], op0=ALU.mult, op1=ALU.add)
+        nc.vector.scalar_tensor_tensor(
+            out=res[:], in0=t1[:], scalar=-float(L // 2), in1=wneg[:], op0=ALU.add, op1=ALU.subtract
+        )
+        nc.sync.dma_start(out=out_v, in_=res[:])

@@ -22,6 +22,7 @@ MANUAL = True
 D1 = 3
 D2 = 2
 E = D1 + D2 + 1
+TX_ON_S = D1
 MCH = 8
 VOLT_CUTS = [0, 2, 4] + list(range(8, NT + 1, 4))
 
@@ -76,7 +77,8 @@ def tile_pinnlayer_pa_t_kernel(tc, Volt, IM, Ybr, n_o_mu_i_u, out):
 
         ssum = const.tile([P, NT], F32, name="ssum")
         qsum = const.tile([P, NT], F32, name="qsum")
-        wneg = const.tile([P, NT], F32, name="wneg")
+        wpos = const.tile([P, NT], F32, name="wpos")
+        qsum_v = const.tile([P, NT], F32, name="qsum_v")
         abs_sb = [const.tile([P, MCH * L // 2], I32, name="absmu%d" % c) for c in range(NT // MCH)]
 
         im_c = const.tile([P, 512], U32, name="im_c", align_bytes=64)
@@ -119,9 +121,9 @@ def tile_pinnlayer_pa_t_kernel(tc, Volt, IM, Ybr, n_o_mu_i_u, out):
                 srcs.append([volt_sb[c][:, j, :].bitcast(F32)[:, u * P:(u + 1) * P] for u in range(2)])
             tps[m] = transpose_pair(srcs, "tp", 2)
 
-        def s_tx(m):
+        def x_tx(m, copy):
             vg = work.tile([P, 1024], BF16, tag="vg", name="vg", bufs=3, align_bytes=64)
-            nc.scalar.copy(
+            copy(
                 out=vg[:].bitcast(F32).rearrange("p (a b u) -> p a b u", a=2, u=2),
                 in_=tps[m][:].rearrange("p a u b -> p a b u"),
             )
@@ -150,12 +152,11 @@ def tile_pinnlayer_pa_t_kernel(tc, Volt, IM, Ybr, n_o_mu_i_u, out):
                     )
                 dvps[m].append(dvp)
 
-        def s_dvx(m):
-            dvg = work.tile([P, 1024], BF16, tag="dvg", name="dvg", bufs=3, align_bytes=64)
-            g = dvg[:].rearrange("p (a b t) -> p a b t", a=2, t=4)
-            for a in range(2):
-                nc.scalar.copy(out=g[:, a], in_=dvps[m][a][:].rearrange("p t b -> p b t"))
-            dvgs[m] = dvg
+        def x_dvx(m, a, copy):
+            if a == 0:
+                dvgs[m] = work.tile([P, 1024], BF16, tag="dvg", name="dvg", bufs=3, align_bytes=64)
+            g = dvgs[m][:].rearrange("p (a b t) -> p a b t", a=2, t=4)
+            copy(out=g[:, a], in_=dvps[m][a][:].rearrange("p t b -> p b t"))
 
         def v_qd(m):
             dc = work.tile([P, 256], U32, tag="dc", name="dc", bufs=D2 + 2, align_bytes=64)
@@ -226,7 +227,13 @@ def tile_pinnlayer_pa_t_kernel(tc, Volt, IM, Ybr, n_o_mu_i_u, out):
                 in1=qts[m][:, a, :],
                 op0=ALU.mult,
                 op1=ALU.max,
-                accum_out=qsum[:, 2 * m + a:2 * m + a + 1],
+                accum_out=qsum_v[:, 2 * m + a:2 * m + a + 1],
+            )
+
+        def s_abs(m, a):
+            junk = work.tile([P, L], F32, tag="junks", name="junks", bufs=2)
+            nc.scalar.activation(
+                out=junk[:], in_=qts[m][:, a, :], func=ACT.Abs, accum_out=qsum[:, 2 * m + a:2 * m + a + 1]
             )
 
         def v_absmu(c):
@@ -238,16 +245,14 @@ def tile_pinnlayer_pa_t_kernel(tc, Volt, IM, Ybr, n_o_mu_i_u, out):
                 op0=ALU.bitwise_and,
             )
 
-        def v_w(tau):
+        def s_w(tau):
             junk = work.tile([P, L], BF16, tag="junk", name="junk", bufs=2)
-            nc.vector.tensor_scalar(
+            nc.scalar.activation(
                 out=junk[:],
-                in0=mu_sb[tau // MCH][:, tau % MCH, :],
-                scalar1=0.0,
-                scalar2=None,
-                op0=ALU.min,
-                op1=ALU.add,
-                accum_out=wneg[:, tau:tau + 1],
+                in_=mu_sb[tau // MCH][:, tau % MCH, :],
+                func=ACT.Relu,
+                scale=-1.0,
+                accum_out=wpos[:, tau:tau + 1],
             )
 
         def ok(m):
@@ -262,25 +267,21 @@ def tile_pinnlayer_pa_t_kernel(tc, Volt, IM, Ybr, n_o_mu_i_u, out):
 
         w_next = [0]
 
-        def mu_work(k):
-            done = []
+        def w_work(k):
             for r in range(k):
-                tau = w_next[0]
-                if tau < NT:
-                    if tau % MCH == 0:
-                        v_absmu(tau // MCH)
-                    v_w(tau)
-                    w_next[0] = tau + 1
-                    done.append(tau)
-            return done
+                if w_next[0] < NT:
+                    s_w(w_next[0])
+                    w_next[0] = w_next[0] + 1
 
+        vcopy = nc.vector.tensor_copy
+        scopy = nc.scalar.copy
         for n in range(NPAIR + E):
+            m = n - E
+            last = m == NPAIR - 1
             if ok(n - D1):
                 pe_s1(n - D1)
-                s_dvx(n - D1)
             if ok(n):
                 pe_tp(n)
-                s_tx(n)
             if n == D1:
                 ytp = [
                     transpose_pair([[y_src(2 * h + a, u) for u in range(2)] for a in range(2)], "ib", 3)
@@ -288,18 +289,33 @@ def tile_pinnlayer_pa_t_kernel(tc, Volt, IM, Ybr, n_o_mu_i_u, out):
                 ]
             if ok(n - D1 - D2):
                 pe_s2(n - D1 - D2)
+            if ok(n):
+                x_tx(n, scopy if n < TX_ON_S else vcopy)
+            if ok(n - D1):
+                x_dvx(n - D1, 0, vcopy)
+                x_dvx(n - D1, 1, vcopy if n >= NPAIR else scopy)
+            if ok(n - D1 - D2):
                 s_sq(n - D1 - D2)
-            m = n - E
-            last = m == NPAIR - 1
             if ok(m) and not last:
                 new_epi_tiles(m)
                 v_i(m, 0, 2)
-            if ok(m - 1):
-                v_abs(m - 1, 0)
+            if ok(n):
+                v_qv(n)
             if ok(m) and not last:
                 v_q(m, 0, 2)
+            if ok(n - D1):
+                v_qd(n - D1)
+            if n == D1:
+                for h in range(2):
+                    exit_pair(vcopy, y_g, h, ytp[h])
+                    quant_half(y_g, y_c, y_s, h)
+            if (n - E + 1) % 4 == 0 and 0 <= (n - E + 1) // 4 < NT // MCH:
+                v_absmu((n - E + 1) // 4)
             if ok(m - 1):
-                v_abs(m - 1, 1)
+                s_abs(m - 1, 0)
+                s_abs(m - 1, 1)
+            if n >= 5:
+                w_work(4 if n < 9 else 2)
             if last:
                 new_epi_tiles(m)
                 v_i(m, 0, 1)
@@ -308,23 +324,15 @@ def tile_pinnlayer_pa_t_kernel(tc, Volt, IM, Ybr, n_o_mu_i_u, out):
                 v_abs(m, 0)
                 v_q(m, 1, 2)
                 v_abs(m, 1)
-            if ok(n - D1):
-                v_qd(n - D1)
-            if n >= 5:
-                mu_work(1)
-            if ok(n):
-                v_qv(n)
-            if n == D1:
-                for h in range(2):
-                    exit_pair(nc.vector.tensor_copy, y_g, h, ytp[h])
-                    quant_half(y_g, y_c, y_s, h)
-            if n >= 5:
-                mu_work(5 if n in (5, 6) else 1)
 
         t1 = const.tile([P, NT], F32, name="t1")
         res = const.tile([P, NT], F32, name="res")
-        nc.vector.scalar_tensor_tensor(out=t1[:], in0=ssum[:], scalar=0.5, in1=qsum[:], op0=ALU.mult, op1=ALU.add)
+        nc.vector.scalar_tensor_tensor(out=t1[:], in0=ssum[:], scalar=0.5, in1=wpos[:], op0=ALU.mult, op1=ALU.add)
+        cut = NT - 2
         nc.vector.scalar_tensor_tensor(
-            out=res[:], in0=t1[:], scalar=-float(L // 2), in1=wneg[:], op0=ALU.add, op1=ALU.subtract
+            out=res[:, 0:cut], in0=t1[:, 0:cut], scalar=-float(L // 2), in1=qsum[:, 0:cut], op0=ALU.add, op1=ALU.add
+        )
+        nc.vector.scalar_tensor_tensor(
+            out=res[:, cut:NT], in0=t1[:, cut:NT], scalar=-float(L // 2), in1=qsum_v[:, cut:NT], op0=ALU.add, op1=ALU.add
         )
         nc.sync.dma_start(out=out_v, in_=res[:])

@@ -11,6 +11,7 @@ I32 = mybir.dt.int32
 FP8X4 = mybir.dt.float8_e4m3fn_x4
 ALU = mybir.AluOpType
 ACT = mybir.ActivationFunctionType
+AX = mybir.AxisListType
 
 B, N2, L2, L = 8192, 512, 512, 256
 P = 128
@@ -23,6 +24,10 @@ D1 = 3
 D2 = 2
 E = D1 + D2 + 1
 TX_ON_S = D1
+WRUN = 32
+DVXA_V_EVERY = 6
+MU_FIRST = 5
+MU_GAP = 3
 MCH = 8
 VOLT_CUTS = [0, 2, 4] + list(range(8, NT + 1, 4))
 
@@ -64,13 +69,12 @@ def tile_pinnlayer_pa_t_kernel(tc, Volt, IM, Ybr, n_o_mu_i_u, out):
         load_volt(0)
         load_volt(1)
         load_volt(2)
+        load_mu(0)
         nc.sync.dma_start(out=y_sb[:], in_=Ybr.rearrange("(c r) j -> r c j", r=P))
-        nmu = 0
         for c in range(3, nvc):
             load_volt(c)
-            if nmu < NT // MCH:
-                load_mu(nmu)
-                nmu += 1
+            if c - 2 < NT // MCH:
+                load_mu(c - 2)
 
         ident = const.tile([P, P], F32, name="ident")
         make_identity(nc, ident[:])
@@ -78,6 +82,9 @@ def tile_pinnlayer_pa_t_kernel(tc, Volt, IM, Ybr, n_o_mu_i_u, out):
         ssum = const.tile([P, NT], F32, name="ssum")
         qsum = const.tile([P, NT], F32, name="qsum")
         wpos = const.tile([P, NT], F32, name="wpos")
+        wrelu_sb = {}
+        ident_bf = const.tile([P, P], BF16, name="ident_bf")
+        make_identity(nc, ident_bf[:])
         qsum_v = const.tile([P, NT], F32, name="qsum_v")
         abs_sb = [const.tile([P, MCH * L // 2], I32, name="absmu%d" % c) for c in range(NT // MCH)]
 
@@ -168,7 +175,7 @@ def tile_pinnlayer_pa_t_kernel(tc, Volt, IM, Ybr, n_o_mu_i_u, out):
             dc, ds = dcs[m]
             ibps[m] = []
             for a in range(2):
-                ibp = psum.tile([P, 512], F32, tag="ib", name="ibp", bufs=3)
+                ibp = psum.tile([P, 512], F32, tag="ib", name="ibp", bufs=2)
                 nc.tensor.matmul_mx(
                     out=ibp[:],
                     lhsT=dc[:, a * P:(a + 1) * P].bitcast(FP8X4),
@@ -245,15 +252,29 @@ def tile_pinnlayer_pa_t_kernel(tc, Volt, IM, Ybr, n_o_mu_i_u, out):
                 op0=ALU.bitwise_and,
             )
 
-        def s_w(tau):
-            junk = work.tile([P, L], BF16, tag="junk", name="junk", bufs=2)
-            nc.scalar.activation(
-                out=junk[:],
-                in_=mu_sb[tau // MCH][:, tau % MCH, :],
-                func=ACT.Relu,
-                scale=-1.0,
-                accum_out=wpos[:, tau:tau + 1],
+        wps = {}
+
+        def v_wrelu(c):
+            wrelu_sb[c] = work.tile([P, MCH, L], BF16, tag="wrelu", name="wrelu", bufs=2)
+            nc.vector.tensor_scalar(
+                out=wrelu_sb[c][:], in0=mu_sb[c][:], scalar1=0.0, scalar2=-1.0, op0=ALU.min, op1=ALU.mult
             )
+
+        def pe_wsum(c):
+            wp = psum.tile([P, MCH, WRUN], F32, tag="w", name="wp", bufs=1)
+            nk = L // WRUN
+            for k in range(nk):
+                nc.tensor.matmul(
+                    out=wp[:],
+                    lhsT=ident_bf[:],
+                    rhs=wrelu_sb[c][:, :, k * WRUN:(k + 1) * WRUN],
+                    start=(k == 0),
+                    stop=(k == nk - 1),
+                )
+            wps[c] = wp
+
+        def v_wred(c):
+            nc.vector.tensor_reduce(out=wpos[:, c * MCH:(c + 1) * MCH], in_=wps[c][:], axis=AX.X, op=ALU.add)
 
         def ok(m):
             return 0 <= m < NPAIR
@@ -265,34 +286,34 @@ def tile_pinnlayer_pa_t_kernel(tc, Volt, IM, Ybr, n_o_mu_i_u, out):
                 quant_half(im_g, im_c, im_s, 0)
         quant_half(im_g, im_c, im_s, 1)
 
-        w_next = [0]
-
-        def w_work(k):
-            for r in range(k):
-                if w_next[0] < NT:
-                    s_w(w_next[0])
-                    w_next[0] = w_next[0] + 1
-
         vcopy = nc.vector.tensor_copy
         scopy = nc.scalar.copy
+        def chunk_at(n, first):
+            c = n - first
+            if c >= 0 and c % MU_GAP == 0 and c // MU_GAP < NT // MCH:
+                return c // MU_GAP
+            return -1
+
         for n in range(NPAIR + E):
             m = n - E
             last = m == NPAIR - 1
-            if ok(n - D1):
-                pe_s1(n - D1)
             if ok(n):
                 pe_tp(n)
+            if ok(n - D1):
+                pe_s1(n - D1)
             if n == D1:
                 ytp = [
-                    transpose_pair([[y_src(2 * h + a, u) for u in range(2)] for a in range(2)], "ib", 3)
+                    transpose_pair([[y_src(2 * h + a, u) for u in range(2)] for a in range(2)], "ib", 2)
                     for h in range(2)
                 ]
             if ok(n - D1 - D2):
                 pe_s2(n - D1 - D2)
+            if chunk_at(n, MU_FIRST + 3) >= 0:
+                pe_wsum(chunk_at(n, MU_FIRST + 3))
             if ok(n):
                 x_tx(n, scopy if n < TX_ON_S else vcopy)
             if ok(n - D1):
-                x_dvx(n - D1, 0, vcopy)
+                x_dvx(n - D1, 0, vcopy if (n >= NPAIR or n % DVXA_V_EVERY == 0) else scopy)
                 x_dvx(n - D1, 1, vcopy if n >= NPAIR else scopy)
             if ok(n - D1 - D2):
                 s_sq(n - D1 - D2)
@@ -308,14 +329,17 @@ def tile_pinnlayer_pa_t_kernel(tc, Volt, IM, Ybr, n_o_mu_i_u, out):
             if n == D1:
                 for h in range(2):
                     exit_pair(vcopy, y_g, h, ytp[h])
+                for h in range(2):
                     quant_half(y_g, y_c, y_s, h)
-            if (n - E + 1) % 4 == 0 and 0 <= (n - E + 1) // 4 < NT // MCH:
-                v_absmu((n - E + 1) // 4)
+            if chunk_at(n, MU_FIRST) >= 0:
+                v_absmu(chunk_at(n, MU_FIRST))
+            if chunk_at(n, MU_FIRST + 1) >= 0:
+                v_wrelu(chunk_at(n, MU_FIRST + 1))
+            if chunk_at(n, MU_FIRST + 5) >= 0:
+                v_wred(chunk_at(n, MU_FIRST + 5))
             if ok(m - 1):
                 s_abs(m - 1, 0)
                 s_abs(m - 1, 1)
-            if n >= 5:
-                w_work(4 if n < 9 else 2)
             if last:
                 new_epi_tiles(m)
                 v_i(m, 0, 1)

@@ -19,11 +19,12 @@ NT = B // P
 NPAIR = NT // 2
 FLOPS = 2 * B * N2 * L2 + 2 * B * L2 * L2
 
-MANUAL = True
+MANUAL = False
 D1 = 3
 D2 = 2
 E = D1 + D2 + 1
 TX_ON_S = D1
+Y_STEP = 1
 WRUN = 32
 DVXA_V_EVERY = 6
 MU_FIRST = 5
@@ -47,10 +48,13 @@ def tile_pinnlayer_pa_t_kernel(tc, Volt, IM, Ybr, n_o_mu_i_u, out):
         psum = ctx.enter_context(tc.psum_pool(name="psum", bufs=2))
 
         im_sb = [const.tile([P, 2, N2], BF16, name="im_sb%d" % h) for h in range(2)]
-        y_sb = const.tile([P, 4, L2], BF16, name="y_sb")
+        y_sb = work.tile([P, 4, L2], BF16, tag="wrelu", name="y_sb", bufs=1)
         nvc = len(VOLT_CUTS) - 1
         volt_sb = [
-            const.tile([P, VOLT_CUTS[c + 1] - VOLT_CUTS[c], N2], BF16, name="volt%d" % c) for c in range(nvc)
+            work.tile([P, 4, N2], BF16, tag="abs", name="volt%d" % c, bufs=2, align_bytes=64)
+            if c == 3
+            else const.tile([P, VOLT_CUTS[c + 1] - VOLT_CUTS[c], N2], BF16, name="volt%d" % c)
+            for c in range(nvc)
         ]
         volt_of = {}
         for c in range(nvc):
@@ -67,14 +71,14 @@ def tile_pinnlayer_pa_t_kernel(tc, Volt, IM, Ybr, n_o_mu_i_u, out):
         for h in range(2):
             nc.sync.dma_start(out=im_sb[h][:], in_=im_v[:, 2 * h:2 * h + 2, :])
         load_volt(0)
+        nc.sync.dma_start(out=y_sb[:], in_=Ybr.rearrange("(c r) j -> r c j", r=P))
         load_volt(1)
         load_volt(2)
-        load_mu(0)
-        nc.sync.dma_start(out=y_sb[:], in_=Ybr.rearrange("(c r) j -> r c j", r=P))
-        for c in range(3, nvc):
+        load_volt(3)
+        for c in range(4, nvc):
             load_volt(c)
-            if c - 2 < NT // MCH:
-                load_mu(c - 2)
+            if c - 4 < NT // MCH:
+                load_mu(c - 4)
 
         ident = const.tile([P, P], F32, name="ident")
         make_identity(nc, ident[:])
@@ -86,14 +90,14 @@ def tile_pinnlayer_pa_t_kernel(tc, Volt, IM, Ybr, n_o_mu_i_u, out):
         ident_bf = const.tile([P, P], BF16, name="ident_bf")
         make_identity(nc, ident_bf[:])
         qsum_v = const.tile([P, NT], F32, name="qsum_v")
-        abs_sb = [const.tile([P, MCH * L // 2], I32, name="absmu%d" % c) for c in range(NT // MCH)]
+        abs_sb = {}
 
         im_c = const.tile([P, 512], U32, name="im_c", align_bytes=64)
         im_s = const.tile([P, 512], U8, name="im_s", align_bytes=64)
         y_c = const.tile([P, 512], U32, name="y_c", align_bytes=64)
         y_s = const.tile([P, 512], U8, name="y_s", align_bytes=64)
         im_g = const.tile([P, 2048], BF16, name="im_g", align_bytes=64)
-        y_g = const.tile([P, 2048], BF16, name="y_g", align_bytes=64)
+        y_g = work.tile([P, 2048], BF16, tag="abs", name="y_g", bufs=2, align_bytes=64)
 
         def transpose_pair(srcs, tag, bufs):
             tp = psum.tile([P, 2, 2, P], F32, tag=tag, name="tp_" + tag, bufs=bufs)
@@ -244,6 +248,7 @@ def tile_pinnlayer_pa_t_kernel(tc, Volt, IM, Ybr, n_o_mu_i_u, out):
             )
 
         def v_absmu(c):
+            abs_sb[c] = work.tile([P, MCH * L // 2], I32, tag="abs", name="absmu", bufs=2, align_bytes=64)
             nc.vector.tensor_scalar(
                 out=abs_sb[c][:],
                 in0=mu_sb[c][:].rearrange("p j l -> p (j l)").bitcast(I32),
@@ -255,7 +260,7 @@ def tile_pinnlayer_pa_t_kernel(tc, Volt, IM, Ybr, n_o_mu_i_u, out):
         wps = {}
 
         def v_wrelu(c):
-            wrelu_sb[c] = work.tile([P, MCH, L], BF16, tag="wrelu", name="wrelu", bufs=2)
+            wrelu_sb[c] = work.tile([P, MCH, L], BF16, tag="wrelu", name="wrelu", bufs=1)
             nc.vector.tensor_scalar(
                 out=wrelu_sb[c][:], in0=mu_sb[c][:], scalar1=0.0, scalar2=-1.0, op0=ALU.min, op1=ALU.mult
             )
@@ -301,7 +306,7 @@ def tile_pinnlayer_pa_t_kernel(tc, Volt, IM, Ybr, n_o_mu_i_u, out):
                 pe_tp(n)
             if ok(n - D1):
                 pe_s1(n - D1)
-            if n == D1:
+            if n == Y_STEP:
                 ytp = [
                     transpose_pair([[y_src(2 * h + a, u) for u in range(2)] for a in range(2)], "ib", 2)
                     for h in range(2)
@@ -326,7 +331,7 @@ def tile_pinnlayer_pa_t_kernel(tc, Volt, IM, Ybr, n_o_mu_i_u, out):
                 v_q(m, 0, 2)
             if ok(n - D1):
                 v_qd(n - D1)
-            if n == D1:
+            if n == Y_STEP:
                 for h in range(2):
                     exit_pair(vcopy, y_g, h, ytp[h])
                 for h in range(2):

@@ -25,7 +25,7 @@ D2 = 2
 E = D1 + D2 + 1
 TX_ON_S = D1
 Y_STEP = 1
-WRUN = 32
+WRUN = 16
 DVXA_V_EVERY = 6
 MU_FIRST = 5
 MU_GAP = 3
@@ -46,6 +46,10 @@ def tile_pinnlayer_pa_t_kernel(tc, Volt, IM, Ybr, n_o_mu_i_u, out):
         const = ctx.enter_context(tc.tile_pool(name="const", bufs=1))
         work = ctx.enter_context(tc.tile_pool(name="work", bufs=2))
         psum = ctx.enter_context(tc.psum_pool(name="psum", bufs=2))
+
+        warm = const.tile([P, 2], F32, name="warm")
+        nc.vector.memset(warm[:, 0:1], 0.0)
+        nc.scalar.activation(out=warm[:, 1:2], in_=warm[:, 0:1], func=ACT.Abs)
 
         im_sb = [const.tile([P, 2, N2], BF16, name="im_sb%d" % h) for h in range(2)]
         y_sb = work.tile([P, 4, L2], BF16, tag="wrelu", name="y_sb", bufs=1)

@@ -26,11 +26,15 @@ E = D1 + D2 + 1
 TX_ON_S = D1
 Y_STEP = 1
 WRUN = 16
-DVXA_V_EVERY = 6
+DVXA_V_EVERY = 4
 MU_FIRST = 5
 MU_GAP = 3
 MCH = 8
 VOLT_CUTS = [0, 2, 4] + list(range(8, NT + 1, 4))
+
+
+def both_ways(c):
+    return c % 2 == 1
 
 
 def tile_pinnlayer_pa_t_kernel(tc, Volt, IM, Ybr, n_o_mu_i_u, out):
@@ -93,6 +97,10 @@ def tile_pinnlayer_pa_t_kernel(tc, Volt, IM, Ybr, n_o_mu_i_u, out):
         wrelu_sb = {}
         ident_bf = const.tile([P, P], BF16, name="ident_bf")
         make_identity(nc, ident_bf[:])
+        half = const.tile([P, P], BF16, name="half")
+        nhalf = const.tile([P, P], BF16, name="nhalf")
+        nc.vector.tensor_scalar(out=half[:], in0=ident_bf[:], scalar1=0.5, scalar2=None, op0=ALU.mult)
+        nc.vector.tensor_scalar(out=nhalf[:], in0=ident_bf[:], scalar1=-0.5, scalar2=None, op0=ALU.mult)
         qsum_v = const.tile([P, NT], F32, name="qsum_v")
         abs_sb = {}
 
@@ -154,7 +162,7 @@ def tile_pinnlayer_pa_t_kernel(tc, Volt, IM, Ybr, n_o_mu_i_u, out):
             vc, vs = vcs[m]
             dvps[m] = []
             for a in range(2):
-                dvp = psum.tile([P, 4, P], F32, tag="dv", name="dvp", bufs=3)
+                dvp = psum.tile([P, 4, P], F32, tag="dv", name="dvp", bufs=4)
                 for t in range(4):
                     nc.tensor.matmul_mx(
                         out=dvp[:, t, :],
@@ -270,15 +278,16 @@ def tile_pinnlayer_pa_t_kernel(tc, Volt, IM, Ybr, n_o_mu_i_u, out):
             )
 
         def pe_wsum(c):
-            wp = psum.tile([P, MCH, WRUN], F32, tag="w", name="wp", bufs=1)
-            nk = L // WRUN
-            for k in range(nk):
+            wp = psum.tile([P, MCH, WRUN], F32, tag="dv", name="wp", bufs=4)
+            if both_ways(c):
+                am = abs_sb[c][:].bitcast(BF16).rearrange("p (j l) -> p j l", l=L)
+                terms = [(half, am), (nhalf, mu_sb[c][:])]
+            else:
+                terms = [(ident_bf, wrelu_sb[c][:])]
+            runs = [(w, x[:, :, k * WRUN:(k + 1) * WRUN]) for w, x in terms for k in range(L // WRUN)]
+            for i in range(len(runs)):
                 nc.tensor.matmul(
-                    out=wp[:],
-                    lhsT=ident_bf[:],
-                    rhs=wrelu_sb[c][:, :, k * WRUN:(k + 1) * WRUN],
-                    start=(k == 0),
-                    stop=(k == nk - 1),
+                    out=wp[:], lhsT=runs[i][0][:], rhs=runs[i][1], start=(i == 0), stop=(i == len(runs) - 1)
                 )
             wps[c] = wp
 
@@ -289,7 +298,7 @@ def tile_pinnlayer_pa_t_kernel(tc, Volt, IM, Ybr, n_o_mu_i_u, out):
             return 0 <= m < NPAIR
 
         for h in range(2):
-            tp = transpose_pair([[im_src(2 * h + a, u) for u in range(2)] for a in range(2)], "dv", 3)
+            tp = transpose_pair([[im_src(2 * h + a, u) for u in range(2)] for a in range(2)], "dv", 4)
             exit_pair(nc.vector.tensor_copy if h == 0 else nc.scalar.copy, im_g, h, tp)
             if h == 0:
                 quant_half(im_g, im_c, im_s, 0)
@@ -342,7 +351,7 @@ def tile_pinnlayer_pa_t_kernel(tc, Volt, IM, Ybr, n_o_mu_i_u, out):
                     quant_half(y_g, y_c, y_s, h)
             if chunk_at(n, MU_FIRST) >= 0:
                 v_absmu(chunk_at(n, MU_FIRST))
-            if chunk_at(n, MU_FIRST + 1) >= 0:
+            if chunk_at(n, MU_FIRST + 1) >= 0 and not both_ways(chunk_at(n, MU_FIRST + 1)):
                 v_wrelu(chunk_at(n, MU_FIRST + 1))
             if chunk_at(n, MU_FIRST + 5) >= 0:
                 v_wred(chunk_at(n, MU_FIRST + 5))

@@ -42,7 +42,7 @@ def tile_pinnlayer_pa_t_kernel(tc, Volt, IM, Ybr, n_o_mu_i_u, out):
     volt_v = Volt.rearrange("(p t) n -> p t n", t=NT)
     mu_v = n_o_mu_i_u.rearrange("(p t) l -> p t l", t=NT)
     out_v = out.rearrange("(p t) -> p t", t=NT)
-    im_v = IM.rearrange("(m t) n -> m t n", t=4)
+    im_v = IM.rearrange("(u m e) n -> m u e n", u=2, e=2)
 
     with ExitStack() as ctx:
         if MANUAL:
@@ -77,7 +77,7 @@ def tile_pinnlayer_pa_t_kernel(tc, Volt, IM, Ybr, n_o_mu_i_u, out):
             nc.sync.dma_start(out=mu_sb[c][:], in_=mu_v[:, c * MCH:(c + 1) * MCH, :])
 
         for h in range(2):
-            nc.sync.dma_start(out=im_sb[h][:], in_=im_v[:, 2 * h:2 * h + 2, :])
+            nc.sync.dma_start(out=im_sb[h][:], in_=im_v[:, h])
         load_volt(0)
         nc.sync.dma_start(out=y_sb[:], in_=Ybr.rearrange("(c r) j -> r c j", r=P))
         load_volt(1)
@@ -133,7 +133,7 @@ def tile_pinnlayer_pa_t_kernel(tc, Volt, IM, Ybr, n_o_mu_i_u, out):
             return im_sb[t // 2][:, t % 2, :].bitcast(F32)[:, u * P:(u + 1) * P]
 
         def y_src(c, u):
-            return y_sb[:, c, :].bitcast(F32).rearrange("p (q u) -> p u q", u=2)[:, u, :]
+            return y_sb[:, c, :].bitcast(F32)[:, u * P:(u + 1) * P]
 
         tps, vgs, vcs, dvps, dvgs, dcs, ibps, sqs, its, qts = {}, {}, {}, {}, {}, {}, {}, {}, {}, {}
 

@@ -23,14 +23,19 @@ MANUAL = False
 D1 = 3
 D2 = 2
 E = D1 + D2 + 1
-TX_ON_S = D1
+TX_ON_S = 5
 Y_STEP = 1
 WRUN = 16
-DVXA_V_EVERY = 4
+DVXA_V_EVERY = 3
 MU_FIRST = 5
+TT = 6
 MU_GAP = 3
 MCH = 8
 VOLT_CUTS = [0, 2, 4] + list(range(8, NT + 1, 4))
+
+
+def twice_turned(m):
+    return m % TT == 2 and m < NPAIR - 3
 
 
 def both_ways(c):
@@ -59,7 +64,7 @@ def tile_pinnlayer_pa_t_kernel(tc, Volt, IM, Ybr, n_o_mu_i_u, out):
         y_sb = work.tile([P, 4, L2], BF16, tag="wrelu", name="y_sb", bufs=1)
         nvc = len(VOLT_CUTS) - 1
         volt_sb = [
-            work.tile([P, 4, N2], BF16, tag="abs", name="volt%d" % c, bufs=2, align_bytes=64)
+            work.tile([P, 4, N2], BF16, tag="abs", name="volt%d" % c, bufs=3, align_bytes=64)
             if c == 3
             else const.tile([P, VOLT_CUTS[c + 1] - VOLT_CUTS[c], N2], BF16, name="volt%d" % c)
             for c in range(nvc)
@@ -101,7 +106,8 @@ def tile_pinnlayer_pa_t_kernel(tc, Volt, IM, Ybr, n_o_mu_i_u, out):
         nhalf = const.tile([P, P], BF16, name="nhalf")
         nc.vector.tensor_scalar(out=half[:], in0=ident_bf[:], scalar1=0.5, scalar2=None, op0=ALU.mult)
         nc.vector.tensor_scalar(out=nhalf[:], in0=ident_bf[:], scalar1=-0.5, scalar2=None, op0=ALU.mult)
-        qsum_v = const.tile([P, NT], F32, name="qsum_v")
+        neg1 = const.tile([P, 1], F32, name="neg1")
+        nc.vector.memset(neg1[:], -1.0)
         abs_sb = {}
 
         im_c = const.tile([P, 512], U32, name="im_c", align_bytes=64)
@@ -109,7 +115,7 @@ def tile_pinnlayer_pa_t_kernel(tc, Volt, IM, Ybr, n_o_mu_i_u, out):
         y_c = const.tile([P, 512], U32, name="y_c", align_bytes=64)
         y_s = const.tile([P, 512], U8, name="y_s", align_bytes=64)
         im_g = const.tile([P, 2048], BF16, name="im_g", align_bytes=64)
-        y_g = work.tile([P, 2048], BF16, tag="abs", name="y_g", bufs=2, align_bytes=64)
+        y_g = work.tile([P, 2048], BF16, tag="abs", name="y_g", bufs=3, align_bytes=64)
 
         def transpose_pair(srcs, tag, bufs):
             tp = psum.tile([P, 2, 2, P], F32, tag=tag, name="tp_" + tag, bufs=bufs)
@@ -214,6 +220,51 @@ def tile_pinnlayer_pa_t_kernel(tc, Volt, IM, Ybr, n_o_mu_i_u, out):
                 )
             sqs[m] = sq
 
+        tts, ats, bks = {}, {}, {}
+
+        def pe_tt(m):
+            tt = psum.tile([P, 2, 2, P], F32, tag="dv", name="tt", bufs=4)
+            for a in range(2):
+                for h in range(2):
+                    for ri in range(2):
+                        lo = ri * L + h * P
+                        nc.tensor.matmul(
+                            out=tt[:, a, h, :],
+                            lhsT=sqs[m][:, a, lo:lo + P],
+                            rhs=ident[:],
+                            is_transpose=True,
+                            start=(ri == 0),
+                            stop=(ri == 1),
+                        )
+            tts[m] = tt
+
+        def s_abst(m):
+            at = work.tile([P, 2, 2, P], F32, tag="at", name="at", bufs=2)
+            nc.scalar.activation(out=at[:], in_=tts[m][:], func=ACT.Abs, bias=neg1[:])
+            ats[m] = at
+
+        def pe_back(m):
+            bk = psum.tile([P, 2, 2, P], F32, tag="dv", name="bk", bufs=4)
+            for a in range(2):
+                for h in range(2):
+                    nc.tensor.transpose(bk[:, a, h, :], ats[m][:, a, h, :], ident[:])
+            bks[m] = bk
+
+        def v_qa(m):
+            am = abs_sb[(2 * m) // MCH][:].bitcast(BF16).rearrange("p (j l) -> p j l", l=L)
+            j0 = (2 * m) % MCH
+            for a in range(2):
+                junk = work.tile([P, L], F32, tag="junkf", name="junkf", bufs=2)
+                nc.vector.scalar_tensor_tensor(
+                    out=junk[:],
+                    in0=am[:, j0 + a, :],
+                    scalar=0.5,
+                    in1=bks[m][:, a].rearrange("p h b -> p (h b)"),
+                    op0=ALU.add,
+                    op1=ALU.mult,
+                    accum_out=qsum[:, 2 * m + a:2 * m + a + 1],
+                )
+
         def new_epi_tiles(m):
             its[m] = work.tile([P, 2, L], F32, tag="it", name="it", bufs=2)
             qts[m] = work.tile([P, 2, L], F32, tag="qt", name="qt", bufs=3)
@@ -250,7 +301,7 @@ def tile_pinnlayer_pa_t_kernel(tc, Volt, IM, Ybr, n_o_mu_i_u, out):
                 in1=qts[m][:, a, :],
                 op0=ALU.mult,
                 op1=ALU.max,
-                accum_out=qsum_v[:, 2 * m + a:2 * m + a + 1],
+                accum_out=qsum[:, 2 * m + a:2 * m + a + 1],
             )
 
         def s_abs(m, a):
@@ -260,7 +311,7 @@ def tile_pinnlayer_pa_t_kernel(tc, Volt, IM, Ybr, n_o_mu_i_u, out):
             )
 
         def v_absmu(c):
-            abs_sb[c] = work.tile([P, MCH * L // 2], I32, tag="abs", name="absmu", bufs=2, align_bytes=64)
+            abs_sb[c] = work.tile([P, MCH * L // 2], I32, tag="abs", name="absmu", bufs=3, align_bytes=64)
             nc.vector.tensor_scalar(
                 out=abs_sb[c][:],
                 in0=mu_sb[c][:].rearrange("p j l -> p (j l)").bitcast(I32),
@@ -335,12 +386,17 @@ def tile_pinnlayer_pa_t_kernel(tc, Volt, IM, Ybr, n_o_mu_i_u, out):
                 x_dvx(n - D1, 1, vcopy if n >= NPAIR else scopy)
             if ok(n - D1 - D2):
                 s_sq(n - D1 - D2)
-            if ok(m) and not last:
+            if ok(m) and twice_turned(m):
+                pe_tt(m)
+                s_abst(m)
+            elif ok(m) and not last:
                 new_epi_tiles(m)
                 v_i(m, 0, 2)
             if ok(n):
                 v_qv(n)
-            if ok(m) and not last:
+            if ok(m - 1) and twice_turned(m - 1):
+                pe_back(m - 1)
+            if ok(m) and not last and not twice_turned(m):
                 v_q(m, 0, 2)
             if ok(n - D1):
                 v_qd(n - D1)
@@ -355,26 +411,24 @@ def tile_pinnlayer_pa_t_kernel(tc, Volt, IM, Ybr, n_o_mu_i_u, out):
                 v_wrelu(chunk_at(n, MU_FIRST + 1))
             if chunk_at(n, MU_FIRST + 5) >= 0:
                 v_wred(chunk_at(n, MU_FIRST + 5))
-            if ok(m - 1):
+            if ok(m - 1) and twice_turned(m - 1):
+                v_qa(m - 1)
+            elif ok(m - 1):
                 s_abs(m - 1, 0)
                 s_abs(m - 1, 1)
             if last:
                 new_epi_tiles(m)
                 v_i(m, 0, 1)
-                v_q(m, 0, 1)
                 v_i(m, 1, 2)
-                v_abs(m, 0)
+                v_q(m, 0, 1)
                 v_q(m, 1, 2)
+                s_abs(m, 0)
                 v_abs(m, 1)
 
         t1 = const.tile([P, NT], F32, name="t1")
         res = const.tile([P, NT], F32, name="res")
         nc.vector.scalar_tensor_tensor(out=t1[:], in0=ssum[:], scalar=0.5, in1=wpos[:], op0=ALU.mult, op1=ALU.add)
-        cut = NT - 2
         nc.vector.scalar_tensor_tensor(
-            out=res[:, 0:cut], in0=t1[:, 0:cut], scalar=-float(L // 2), in1=qsum[:, 0:cut], op0=ALU.add, op1=ALU.add
-        )
-        nc.vector.scalar_tensor_tensor(
-            out=res[:, cut:NT], in0=t1[:, cut:NT], scalar=-float(L // 2), in1=qsum_v[:, cut:NT], op0=ALU.add, op1=ALU.add
+            out=res[:], in0=t1[:], scalar=-float(L // 2), in1=qsum[:], op0=ALU.add, op1=ALU.add
         )
         nc.sync.dma_start(out=out_v, in_=res[:])

from contextlib import ExitStack

import concourse.mybir as mybir
from concourse.masks import make_identity

F32 = mybir.dt.float32
BF16 = mybir.dt.bfloat16
U32 = mybir.dt.uint32
U8 = mybir.dt.uint8
I32 = mybir.dt.int32
FP8X4 = mybir.dt.float8_e4m3fn_x4
ALU = mybir.AluOpType
ACT = mybir.ActivationFunctionType
AX = mybir.AxisListType

B, N2, L2, L = 8192, 512, 512, 256
P = 128
NT = B // P
NPAIR = NT // 2
FLOPS = 2 * B * N2 * L2 + 2 * B * L2 * L2

MANUAL = False
D1 = 3
D2 = 2
E = D1 + D2 + 1
TX_ON_S = 5
Y_STEP = 1
WRUN = 16
DVXA_V_EVERY = 3
MU_FIRST = 5
TT = 6
MU_GAP = 3
MCH = 8
VOLT_CUTS = [0, 2, 4] + list(range(8, NT + 1, 4))


def twice_turned(m):
    return m % TT == 2 and m < NPAIR - 3


def both_ways(c):
    return c % 2 == 1


def tile_pinnlayer_pa_t_kernel(tc, Volt, IM, Ybr, n_o_mu_i_u, out):
    nc = tc.nc
    volt_v = Volt.rearrange("(p t) n -> p t n", t=NT)
    mu_v = n_o_mu_i_u.rearrange("(p t) l -> p t l", t=NT)
    out_v = out.rearrange("(p t) -> p t", t=NT)
    im_v = IM.rearrange("(u m e) n -> m u e n", u=2, e=2)

    with ExitStack() as ctx:
        if MANUAL:
            ctx.enter_context(tc.manual_schedule())
        const = ctx.enter_context(tc.tile_pool(name="const", bufs=1))
        work = ctx.enter_context(tc.tile_pool(name="work", bufs=2))
        psum = ctx.enter_context(tc.psum_pool(name="psum", bufs=2))

        warm = const.tile([P, 2], F32, name="warm")
        nc.vector.memset(warm[:, 0:1], 0.0)
        nc.scalar.activation(out=warm[:, 1:2], in_=warm[:, 0:1], func=ACT.Abs)

        im_sb = [const.tile([P, 2, N2], BF16, name="im_sb%d" % h) for h in range(2)]
        y_sb = work.tile([P, 4, L2], BF16, tag="wrelu", name="y_sb", bufs=1)
        nvc = len(VOLT_CUTS) - 1
        volt_sb = [
            work.tile([P, 4, N2], BF16, tag="abs", name="volt%d" % c, bufs=3, align_bytes=64)
            if c == 3
            else const.tile([P, VOLT_CUTS[c + 1] - VOLT_CUTS[c], N2], BF16, name="volt%d" % c)
            for c in range(nvc)
        ]
        volt_of = {}
        for c in range(nvc):
            for j in range(VOLT_CUTS[c + 1] - VOLT_CUTS[c]):
                volt_of[VOLT_CUTS[c] + j] = (c, j)
        mu_sb = [const.tile([P, MCH, L], BF16, name="mu%d" % c) for c in range(NT // MCH)]

        def load_volt(c):
            nc.sync.dma_start(out=volt_sb[c][:], in_=volt_v[:, VOLT_CUTS[c]:VOLT_CUTS[c + 1], :])

        def load_mu(c):
            nc.sync.dma_start(out=mu_sb[c][:], in_=mu_v[:, c * MCH:(c + 1) * MCH, :])

        for h in range(2):
            nc.sync.dma_start(out=im_sb[h][:], in_=im_v[:, h])
        load_volt(0)
        nc.sync.dma_start(out=y_sb[:], in_=Ybr.rearrange("(c r) j -> r c j", r=P))
        load_volt(1)
        load_volt(2)
        load_volt(3)
        for c in range(4, nvc):
            load_volt(c)
            if c - 4 < NT // MCH:
                load_mu(c - 4)

        ident = const.tile([P, P], F32, name="ident")
        make_identity(nc, ident[:])

        ssum = const.tile([P, NT], F32, name="ssum")
        qsum = const.tile([P, NT], F32, name="qsum")
        wpos = const.tile([P, NT], F32, name="wpos")
        wrelu_sb = {}
        ident_bf = const.tile([P, P], BF16, name="ident_bf")
        make_identity(nc, ident_bf[:])
        half = const.tile([P, P], BF16, name="half")
        nhalf = const.tile([P, P], BF16, name="nhalf")
        nc.vector.tensor_scalar(out=half[:], in0=ident_bf[:], scalar1=0.5, scalar2=None, op0=ALU.mult)
        nc.vector.tensor_scalar(out=nhalf[:], in0=ident_bf[:], scalar1=-0.5, scalar2=None, op0=ALU.mult)
        neg1 = const.tile([P, 1], F32, name="neg1")
        nc.vector.memset(neg1[:], -1.0)
        abs_sb = {}

        im_c = const.tile([P, 512], U32, name="im_c", align_bytes=64)
        im_s = const.tile([P, 512], U8, name="im_s", align_bytes=64)
        y_c = const.tile([P, 512], U32, name="y_c", align_bytes=64)
        y_s = const.tile([P, 512], U8, name="y_s", align_bytes=64)
        im_g = const.tile([P, 2048], BF16, name="im_g", align_bytes=64)
        y_g = work.tile([P, 2048], BF16, tag="abs", name="y_g", bufs=3, align_bytes=64)

        def transpose_pair(srcs, tag, bufs):
            tp = psum.tile([P, 2, 2, P], F32, tag=tag, name="tp_" + tag, bufs=bufs)
            for a in range(2):
                for u in range(2):
                    nc.tensor.transpose(tp[:, a, u, :], srcs[a][u], ident[:])
            return tp

        def exit_pair(eng_copy, grouped, h, tp):
            g32 = grouped[:].bitcast(F32).rearrange("p (t m u) -> p t m u", t=4, u=2)
            eng_copy(out=g32[:, 2 * h:2 * h + 2], in_=tp[:].rearrange("p a u m -> p a m u"))

        def quant_half(grouped, codes, scales, h):
            nc.vector.quantize_mx(
                out=codes[:, 256 * h:256 * h + 256].bitcast(FP8X4),
                scales=scales[:, 256 * h:256 * h + 256],
                in_=grouped[:, 1024 * h:1024 * h + 1024],
            )

        def im_src(t, u):
            return im_sb[t // 2][:, t % 2, :].bitcast(F32)[:, u * P:(u + 1) * P]

        def y_src(c, u):
            return y_sb[:, c, :].bitcast(F32)[:, u * P:(u + 1) * P]

        tps, vgs, vcs, dvps, dvgs, dcs, ibps, sqs, its, qts = {}, {}, {}, {}, {}, {}, {}, {}, {}, {}

        def pe_tp(m):
            srcs = []
            for a in range(2):
                c, j = volt_of[2 * m + a]
                srcs.append([volt_sb[c][:, j, :].bitcast(F32)[:, u * P:(u + 1) * P] for u in range(2)])
            tps[m] = transpose_pair(srcs, "tp", 2)

        def x_tx(m, copy):
            vg = work.tile([P, 1024], BF16, tag="vg", name="vg", bufs=3, align_bytes=64)
            copy(
                out=vg[:].bitcast(F32).rearrange("p (a b u) -> p a b u", a=2, u=2),
                in_=tps[m][:].rearrange("p a u b -> p a b u"),
            )
            vgs[m] = vg

        def v_qv(m):
            vc = work.tile([P, 256], U32, tag="vc", name="vc", bufs=D1 + 2, align_bytes=64)
            vs = work.tile([P, 256], U8, tag="vs", name="vs", bufs=D1 + 2, align_bytes=64)
            nc.vector.quantize_mx(out=vc[:].bitcast(FP8X4), scales=vs[:], in_=vgs[m][:])
            vcs[m] = (vc, vs)

        def pe_s1(m):
            vc, vs = vcs[m]
            dvps[m] = []
            for a in range(2):
                dvp = psum.tile([P, 4, P], F32, tag="dv", name="dvp", bufs=4)
                for t in range(4):
                    nc.tensor.matmul_mx(
                        out=dvp[:, t, :],
                        lhsT=im_c[:, t * P:(t + 1) * P].bitcast(FP8X4),
                        lhsT_scale=im_s[:, t * P:(t + 1) * P],
                        rhs=vc[:, a * P:(a + 1) * P].bitcast(FP8X4),
                        rhs_scale=vs[:, a * P:(a + 1) * P],
                        start=True,
                        stop=True,
                    )
                dvps[m].append(dvp)

        def x_dvx(m, a, copy):
            if a == 0:
                dvgs[m] = work.tile([P, 1024], BF16, tag="dvg", name="dvg", bufs=3, align_bytes=64)
            g = dvgs[m][:].rearrange("p (a b t) -> p a b t", a=2, t=4)
            copy(out=g[:, a], in_=dvps[m][a][:].rearrange("p t b -> p b t"))

        def v_qd(m):
            dc = work.tile([P, 256], U32, tag="dc", name="dc", bufs=D2 + 2, align_bytes=64)
            ds = work.tile([P, 256], U8, tag="ds", name="ds", bufs=D2 + 2, align_bytes=64)
            nc.vector.quantize_mx(out=dc[:].bitcast(FP8X4), scales=ds[:], in_=dvgs[m][:])
            dcs[m] = (dc, ds)

        def pe_s2(m):
            dc, ds = dcs[m]
            ibps[m] = []
            for a in range(2):
                ibp = psum.tile([P, 512], F32, tag="ib", name="ibp", bufs=2)
                nc.tensor.matmul_mx(
                    out=ibp[:],
                    lhsT=dc[:, a * P:(a + 1) * P].bitcast(FP8X4),
                    lhsT_scale=ds[:, a * P:(a + 1) * P],
                    rhs=y_c[:].bitcast(FP8X4),
                    rhs_scale=y_s[:],
                    start=True,
                    stop=True,
                )
                ibps[m].append(ibp)

        def s_sq(m):
            sq = work.tile([P, 2, 512], F32, tag="sq", name="sq", bufs=3)
            for a in range(2):
                nc.scalar.activation(
                    out=sq[:, a, :],
                    in_=ibps[m][a][:],
                    func=ACT.Square,
                    accum_out=ssum[:, 2 * m + a:2 * m + a + 1],
                )
            sqs[m] = sq

        tts, ats, bks = {}, {}, {}

        def pe_tt(m):
            tt = psum.tile([P, 2, 2, P], F32, tag="dv", name="tt", bufs=4)
            for a in range(2):
                for h in range(2):
                    for ri in range(2):
                        lo = ri * L + h * P
                        nc.tensor.matmul(
                            out=tt[:, a, h, :],
                            lhsT=sqs[m][:, a, lo:lo + P],
                            rhs=ident[:],
                            is_transpose=True,
                            start=(ri == 0),
                            stop=(ri == 1),
                        )
            tts[m] = tt

        def s_abst(m):
            at = work.tile([P, 2, 2, P], F32, tag="at", name="at", bufs=2)
            nc.scalar.activation(out=at[:], in_=tts[m][:], func=ACT.Abs, bias=neg1[:])
            ats[m] = at

        def pe_back(m):
            bk = psum.tile([P, 2, 2, P], F32, tag="dv", name="bk", bufs=4)
            for a in range(2):
                for h in range(2):
                    nc.tensor.transpose(bk[:, a, h, :], ats[m][:, a, h, :], ident[:])
            bks[m] = bk

        def v_qa(m):
            am = abs_sb[(2 * m) // MCH][:].bitcast(BF16).rearrange("p (j l) -> p j l", l=L)
            j0 = (2 * m) % MCH
            for a in range(2):
                junk = work.tile([P, L], F32, tag="junkf", name="junkf", bufs=2)
                nc.vector.scalar_tensor_tensor(
                    out=junk[:],
                    in0=am[:, j0 + a, :],
                    scalar=0.5,
                    in1=bks[m][:, a].rearrange("p h b -> p (h b)"),
                    op0=ALU.add,
                    op1=ALU.mult,
                    accum_out=qsum[:, 2 * m + a:2 * m + a + 1],
                )

        def new_epi_tiles(m):
            its[m] = work.tile([P, 2, L], F32, tag="it", name="it", bufs=2)
            qts[m] = work.tile([P, 2, L], F32, tag="qt", name="qt", bufs=3)

        def v_i(m, lo, hi):
            sq = sqs[m]
            nc.vector.scalar_tensor_tensor(
                out=its[m][:, lo:hi, :],
                in0=sq[:, lo:hi, 0:L],
                scalar=-1.0,
                in1=sq[:, lo:hi, L:2 * L],
                op0=ALU.add,
                op1=ALU.add,
            )

        def v_q(m, lo, hi):
            am = abs_sb[(2 * m) // MCH][:].bitcast(BF16).rearrange("p (j l) -> p j l", l=L)
            j0 = (2 * m) % MCH
            nc.vector.scalar_tensor_tensor(
                out=qts[m][:, lo:hi, :],
                in0=am[:, j0 + lo:j0 + hi, :],
                scalar=0.5,
                in1=its[m][:, lo:hi, :],
                op0=ALU.add,
                op1=ALU.mult,
            )

        def v_abs(m, a):
            junk = work.tile([P, L], F32, tag="junkf", name="junkf", bufs=2)
            nc.vector.scalar_tensor_tensor(
                out=junk[:],
                in0=qts[m][:, a, :],
                scalar=-1.0,
                in1=qts[m][:, a, :],
                op0=ALU.mult,
                op1=ALU.max,
                accum_out=qsum[:, 2 * m + a:2 * m + a + 1],
            )

        def s_abs(m, a):
            junk = work.tile([P, L], F32, tag="junks", name="junks", bufs=2)
            nc.scalar.activation(
                out=junk[:], in_=qts[m][:, a, :], func=ACT.Abs, accum_out=qsum[:, 2 * m + a:2 * m + a + 1]
            )

        def v_absmu(c):
            abs_sb[c] = work.tile([P, MCH * L // 2], I32, tag="abs", name="absmu", bufs=3, align_bytes=64)
            nc.vector.tensor_scalar(
                out=abs_sb[c][:],
                in0=mu_sb[c][:].rearrange("p j l -> p (j l)").bitcast(I32),
                scalar1=0x7FFF7FFF,
                scalar2=None,
                op0=ALU.bitwise_and,
            )

        wps = {}

        def v_wrelu(c):
            wrelu_sb[c] = work.tile([P, MCH, L], BF16, tag="wrelu", name="wrelu", bufs=1)
            nc.vector.tensor_scalar(
                out=wrelu_sb[c][:], in0=mu_sb[c][:], scalar1=0.0, scalar2=-1.0, op0=ALU.min, op1=ALU.mult
            )

        def pe_wsum(c):
            wp = psum.tile([P, MCH, WRUN], F32, tag="dv", name="wp", bufs=4)
            if both_ways(c):
                am = abs_sb[c][:].bitcast(BF16).rearrange("p (j l) -> p j l", l=L)
                terms = [(half, am), (nhalf, mu_sb[c][:])]
            else:
                terms = [(ident_bf, wrelu_sb[c][:])]
            runs = [(w, x[:, :, k * WRUN:(k + 1) * WRUN]) for w, x in terms for k in range(L // WRUN)]
            for i in range(len(runs)):
                nc.tensor.matmul(
                    out=wp[:], lhsT=runs[i][0][:], rhs=runs[i][1], start=(i == 0), stop=(i == len(runs) - 1)
                )
            wps[c] = wp

        def v_wred(c):
            nc.vector.tensor_reduce(out=wpos[:, c * MCH:(c + 1) * MCH], in_=wps[c][:], axis=AX.X, op=ALU.add)

        def ok(m):
            return 0 <= m < NPAIR

        for h in range(2):
            tp = transpose_pair([[im_src(2 * h + a, u) for u in range(2)] for a in range(2)], "dv", 4)
            exit_pair(nc.vector.tensor_copy if h == 0 else nc.scalar.copy, im_g, h, tp)
            if h == 0:
                quant_half(im_g, im_c, im_s, 0)
        quant_half(im_g, im_c, im_s, 1)

        vcopy = nc.vector.tensor_copy
        scopy = nc.scalar.copy
        def chunk_at(n, first):
            c = n - first
            if c >= 0 and c % MU_GAP == 0 and c // MU_GAP < NT // MCH:
                return c // MU_GAP
            return -1

        for n in range(NPAIR + E):
            m = n - E
            last = m == NPAIR - 1
            if ok(n):
                pe_tp(n)
            if ok(n - D1):
                pe_s1(n - D1)
            if n == Y_STEP:
                ytp = [
                    transpose_pair([[y_src(2 * h + a, u) for u in range(2)] for a in range(2)], "ib", 2)
                    for h in range(2)
                ]
            if ok(n - D1 - D2):
                pe_s2(n - D1 - D2)
            if chunk_at(n, MU_FIRST + 3) >= 0:
                pe_wsum(chunk_at(n, MU_FIRST + 3))
            if ok(n):
                x_tx(n, scopy if n < TX_ON_S else vcopy)
            if ok(n - D1):
                x_dvx(n - D1, 0, vcopy if (n >= NPAIR or n % DVXA_V_EVERY == 0) else scopy)
                x_dvx(n - D1, 1, vcopy if n >= NPAIR else scopy)
            if ok(n - D1 - D2):
                s_sq(n - D1 - D2)
            if ok(m) and twice_turned(m):
                pe_tt(m)
                s_abst(m)
            elif ok(m) and not last:
                new_epi_tiles(m)
                v_i(m, 0, 2)
            if ok(n):
                v_qv(n)
            if ok(m - 1) and twice_turned(m - 1):
                pe_back(m - 1)
            if ok(m) and not last and not twice_turned(m):
                v_q(m, 0, 2)
            if ok(n - D1):
                v_qd(n - D1)
            if n == Y_STEP:
                for h in range(2):
                    exit_pair(vcopy, y_g, h, ytp[h])
                for h in range(2):
                    quant_half(y_g, y_c, y_s, h)
            if chunk_at(n, MU_FIRST) >= 0:
                v_absmu(chunk_at(n, MU_FIRST))
            if chunk_at(n, MU_FIRST + 1) >= 0 and not both_ways(chunk_at(n, MU_FIRST + 1)):
                v_wrelu(chunk_at(n, MU_FIRST + 1))
            if chunk_at(n, MU_FIRST + 5) >= 0:
                v_wred(chunk_at(n, MU_FIRST + 5))
            if ok(m - 1) and twice_turned(m - 1):
                v_qa(m - 1)
            elif ok(m - 1):
                s_abs(m - 1, 0)
                s_abs(m - 1, 1)
            if last:
                new_epi_tiles(m)
                v_i(m, 0, 1)
                v_i(m, 1, 2)
                v_q(m, 0, 1)
                v_q(m, 1, 2)
                s_abs(m, 0)
                v_abs(m, 1)

        t1 = const.tile([P, NT], F32, name="t1")
        res = const.tile([P, NT], F32, name="res")
        nc.vector.scalar_tensor_tensor(out=t1[:], in0=ssum[:], scalar=0.5, in1=wpos[:], op0=ALU.mult, op1=ALU.add)
        nc.vector.scalar_tensor_tensor(
            out=res[:], in0=t1[:], scalar=-float(L // 2), in1=qsum[:], op0=ALU.add, op1=ALU.add
        )
        nc.sync.dma_start(out=out_v, in_=res[:])
